import numpy as np
import ml_dtypes


def mxq(x, axis, fmt="e4m3"):
    dtype, down = {"e4m3": (ml_dtypes.float8_e4m3fn, 7), "e5m2": (ml_dtypes.float8_e5m2, 14)}[fmt]
    v = np.moveaxis(np.asarray(x, np.float32).astype(ml_dtypes.bfloat16).astype(np.float64), axis, -1)
    blocks = v.reshape(v.shape[:-1] + (-1, 32))
    amax = np.abs(blocks).max(-1, keepdims=True)
    byte = np.maximum(np.where(amax > 0, np.frexp(amax)[1] - 1 + 127, 0) - down, 1)
    scale = np.exp2(byte - 127.0)
    codes = (blocks / scale).astype(np.float32).astype(dtype).astype(np.float64)
    return np.moveaxis((codes * scale).reshape(v.shape), -1, axis)


WIDE = False


def mx_kscale(k):
    if not WIDE:
        return np.ones(k)
    levels = np.array([10, -10, 5, -5, 0])
    if k % 512:
        return np.exp2(np.random.permutation(np.resize(levels, k // 32))).repeat(32)
    a = np.empty((k // 512, 16))
    for p in range(k // 512):
        a[p, :8] = np.random.permutation(np.resize(levels, 8))
        for g in range(8):
            far = levels[np.abs(levels - a[p, g]) >= 10]
            a[p, g + 8] = far[np.random.randint(len(far))]
    return np.exp2(a.ravel()).repeat(32)


BF16 = ml_dtypes.bfloat16


def bf(x):
    return np.asarray(x, np.float32).astype(BF16)


def f64(x):
    return np.asarray(x).astype(np.float64)


E2M1 = np.array([0.0, 0.5, 1.0, 1.5, 2.0, 3.0, 4.0, 6.0, -0.0, -0.5, -1.0, -1.5, -2.0, -3.0, -4.0, -6.0])


def pack_weight(w, fmt):
    k, n = w.shape
    w = f64(bf(w)).reshape(k // 32, 32, n)
    amax = np.abs(w).max(1)
    if fmt == "e4m3":
        byte = np.frexp(amax)[1] - 1 + 127 - 7
    else:
        mant, ex = np.frexp(amax / 6.0)
        byte = np.where(mant > 0.5, ex, ex - 1) + 127
    byte = np.clip(np.where(amax > 0, byte, 1), 1, 254)
    scaled = (w * np.exp2(127.0 - byte)[:, None, :]).reshape(k, n).astype(np.float32)
    by_word = np.ascontiguousarray(scaled.reshape(k // 512, 128, 4, n).transpose(0, 1, 3, 2))
    if fmt == "e4m3":
        words = by_word.astype(ml_dtypes.float8_e4m3fn).view(np.uint8)
    else:
        c = by_word.astype(ml_dtypes.float4_e2m1fn).view(np.uint8) & 0xF
        words = c[..., 0::2] | (c[..., 1::2] << 4)
    return np.ascontiguousarray(words), np.ascontiguousarray(byte.astype(np.uint8).reshape(k // 512, 16, n))


def unpack_weight(words, scales, fmt):
    g, p, n, _ = words.shape
    if fmt == "e4m3":
        vals = np.ascontiguousarray(words).view(ml_dtypes.float8_e4m3fn).astype(np.float64)
    else:
        nib = np.empty((g, p, n, 4), np.uint8)
        nib[..., 0::2] = words & 0xF
        nib[..., 1::2] = words >> 4
        vals = E2M1[nib]
    vals = vals * np.repeat(np.exp2(scales.astype(np.float64) - 127.0), 8, axis=1)[..., None]
    return vals.transpose(0, 1, 3, 2).reshape(g * 512, n)
def pack4(w):
    words, scales = pack_weight(w, "e2m1")
    return words.reshape(words.shape[0], 128, -1), scales


def unpack4(words, scales):
    return unpack_weight(words.reshape(words.shape[0], 128, -1, 2), scales, "e2m1")


B, N, C, F = 4, 32, 1024, 1024
KP = 5 * C
EPS_GN = 1e-5


def draw0():
    s = np.concatenate([np.ones(C), mx_kscale(KP - C)])
    t = mx_kscale(C)
    gap = 0.65 * np.sqrt(2.0 * np.log(N))
    mean = 0.65 * np.random.standard_normal((B, N, C))
    lo = mean - gap - 0.35 * np.random.standard_normal((B, N, C))
    hi = mean + gap + 0.35 * np.random.standard_normal((B, N, C))
    std = 0.8 + 0.1 * np.random.standard_normal((B, N, C))
    x = bf(np.random.standard_normal((B, N, C)))
    W_post_words, W_post_scales = pack4(np.random.standard_normal((KP, C)) / np.sqrt(KP) / s[:, None] * t)
    b_post = bf(np.random.standard_normal(C) * 0.5 * t)
    W_lin_words, W_lin_scales = pack4(np.random.standard_normal((C, C)) / np.sqrt(C) / t[:, None])
    return {"x": x,
            "agg": bf(np.concatenate([mean, lo, hi, std], axis=-1) * s[C:]),
            "W_post_words": W_post_words,
            "W_post_scales": W_post_scales,
            "b_post": b_post,
            "W_lin_words": W_lin_words,
            "W_lin_scales": W_lin_scales,
            "b_lin": bf(np.random.standard_normal(C) * 0.5),
            "gn_weight": bf(1.0 + 0.2 * np.random.standard_normal(C)),
            "gn_bias": bf(0.2 * np.random.standard_normal(C)),
            "gn_alpha": bf(0.6 + 0.2 * np.random.standard_normal(C))}


def core(x, agg, W_post_words, W_post_scales, b_post, W_lin_words, W_lin_scales, b_lin, gn_weight, gn_bias, gn_alpha):
    res = f64(x)
    cat = np.concatenate([res, f64(agg)], axis=-1)
    out = (mxq(cat, 2, "e4m3") @ unpack4(W_post_words, W_post_scales)) + f64(b_post)
    out = (mxq(out, 2, "e4m3") @ unpack4(W_lin_words, W_lin_scales)) + f64(b_lin)
    flat = out.reshape(B * N, C)
    mu = flat.mean(axis=0, keepdims=True)
    centered = flat - f64(gn_alpha) * mu
    v = (centered * centered).mean(axis=0, keepdims=True)
    normed = f64(gn_weight) * centered / np.sqrt(v + EPS_GN) + f64(gn_bias)
    return np.maximum(normed, 0.0).reshape(B, N, C) + res


def e4m3fn_bytes(y):
    return np.clip(np.asarray(y, np.float64), -448.0, 448.0).astype(np.float32).astype(ml_dtypes.float8_e4m3fn).view(np.uint8)


def e4m3fn_values(b):
    return np.asarray(b, np.uint8).view(ml_dtypes.float8_e4m3fn).astype(np.float64)


def setup_inputs():
    d = draw0()
    x0 = np.asarray(d['agg']).astype(np.float64)
    s = (np.max(np.abs(x0), axis=(0, 1), keepdims=True) / 448.0).astype(np.float32)
    out = {}
    for k, v in d.items():
        if k == 'agg':
            out['agg_bytes'] = e4m3fn_bytes(x0 / s.astype(np.float64))
            out['agg_scale'] = s
        else:
            out[k] = v
    return out


def reference(x, agg_bytes, agg_scale, W_post_words, W_post_scales, b_post, W_lin_words, W_lin_scales, b_lin, gn_weight, gn_bias, gn_alpha):
    return core(x, e4m3fn_values(agg_bytes) * agg_scale.astype(np.float64), W_post_words, W_post_scales, b_post, W_lin_words, W_lin_scales, b_lin, gn_weight, gn_bias, gn_alpha)

@@ -1,0 +1,374 @@
+from contextlib import ExitStack
+
+import concourse.mybir as mybir
+from concourse.masks import make_identity
+
+F32 = mybir.dt.float32
+BF16 = mybir.dt.bfloat16
+U32 = mybir.dt.uint32
+I32 = mybir.dt.int32
+U8 = mybir.dt.uint8
+E4M3 = mybir.dt.float8_e4m3fn
+E4M3X4 = mybir.dt.float8_e4m3fn_x4
+E2M1X4 = mybir.dt.float4_e2m1fn_x4
+ADD = mybir.AluOpType.add
+MULT = mybir.AluOpType.mult
+MAX = mybir.AluOpType.max
+ACT = mybir.ActivationFunctionType
+
+P = 128
+T = 128
+C = 1024
+GX = 2
+GA = 8
+G = GX + GA
+EPS = 1e-5
+FLOPS = 2 * T * (G * 512 + C) * C
+
+
+def tile_gnnlayer_pb_w4_kernel(tc, x, agg_bytes, agg_scale, W_post_words, W_post_scales, b_post,
+                                           W_lin_words, W_lin_scales, b_lin, gn_weight, gn_bias, gn_alpha, out):
+    nc = tc.nc
+    x_rows = x.rearrange("b n c -> (b n) c")
+    agg_rows = agg_bytes.rearrange("b n k -> (b n) k")
+    out_rows = out.rearrange("b n c -> (b n) c")
+    asc_rows = agg_scale.rearrange("o b (g c) -> (o b g) c", g=GA)
+    wps = W_post_scales.bitcast(I32).rearrange("g (q r) n -> r q g n", r=4)
+    wls = W_lin_scales.bitcast(I32).rearrange("g (q r) n -> r q g n", r=4)
+
+    with ExitStack() as ctx:
+        keep = ctx.enter_context(tc.tile_pool(name="keep", bufs=1))
+        psum = ctx.enter_context(tc.psum_pool(name="psum", bufs=6))
+        ctx.enter_context(tc.manual_schedule())
+
+        def sb(name, shape, dtype):
+            return keep.tile(shape, dtype, name=name, align_bytes=64)
+
+        def bank(name, shape, dtype=F32):
+            return psum.tile(shape, dtype, name=name, tag="bank", bufs=6)
+
+        def acc_bank(name, shape):
+            return psum.tile(shape, F32, name=name, tag="acc", bufs=2)
+
+        asc = sb("asc", [P, 512], F32)
+        warm = sb("warm", [P, 1], F32)
+        warm2 = sb("warm2", [P, 1], F32)
+        ident = sb("ident", [P, P], F32)
+        ident_bf = sb("ident_bf", [P, P], BF16)
+        ones_bf = sb("ones_bf", [P, P], BF16)
+        prow = sb("prow", [P, P], BF16)
+        brow = sb("brow", [P, C], BF16)
+        x_sb = sb("x_sb", [P, C], BF16)
+        agg_u8 = [sb("agg_u8_%d" % i, [P, n], U8) for i, n in enumerate((1024, 1024, 2048))]
+        aggw = sb("aggw", [P, GA, 512], BF16)
+        s_col = sb("s_col", [P, GA, 4], F32)
+        grouped = sb("grouped", [P, G, 512], BF16)
+        codes = sb("codes", [P, G, T], U32)
+        planes = sb("planes", [P, G, T], U8)
+        post_sc = sb("post_sc", [P, G, C], U8)
+        lin_sc = sb("lin_sc", [P, 2, C], U8)
+        post_w = [sb("post_w%d" % i, [P, 2, 2 * C], U8) for i in range(4)]
+        post_wl = [sb("post_wl%d" % h, [P, 2, C], U8) for h in range(2)]
+        lin_w = sb("lin_w", [P, 2, 2 * C], U8)
+
+        nc.gpsimd.memset(brow[:].bitcast(I32), 0)
+        nc.vector.memset(asc[:], 0.0)
+        nc.vector.memset(warm[:], 1.0)
+        nc.vector.memset(ones_bf[:], 1.0)
+        nc.sync.dma_start(out=agg_u8[0][:], in_=agg_rows[:, 0:1024])
+        nc.sync.dma_start(out=asc[0:GA, :], in_=asc_rows)
+        nc.sync.dma_start(out=agg_u8[1][:], in_=agg_rows[:, 1024:2048])
+        nc.sync.dma_start(out=agg_u8[2][:], in_=agg_rows[:, 2048:4096])
+        nc.scalar.dma_start(out=brow[0:1, :], in_=b_post.rearrange("(o c) -> o c", o=1))
+        nc.scalar.activation(out=warm2[:], in_=warm[:], func=ACT.Abs_reciprocal_sqrt)
+        nc.sync.dma_start(out=x_sb[:], in_=x_rows)
+        nc.vector.memset(post_sc[:].bitcast(I32), 0)
+        nc.vector.memset(lin_sc[:].bitcast(I32), 0)
+        for r in range(4):
+            nc.sync.dma_start(out=post_sc[r:128:32, :, :].bitcast(I32), in_=wps[r])
+        for i in (1, 2, 0, 3):
+            nc.sync.dma_start(out=post_w[i][:], in_=W_post_words[2 * i:2 * i + 2].rearrange("g p n -> p g n"))
+        for h in range(2):
+            nc.sync.dma_start(out=post_wl[h][:], in_=W_post_words[8:10, :, h * C:(h + 1) * C].rearrange("g p n -> p g n"))
+        for r in range(4):
+            nc.sync.dma_start(out=lin_sc[r:128:32, :, :].bitcast(I32), in_=wls[r])
+        nc.sync.dma_start(out=lin_w[:], in_=W_lin_words.rearrange("g p n -> p g n"))
+
+        make_identity(nc, ident[:])
+        nc.gpsimd.memset(prow[:], 0.0)
+        for i, vec in enumerate((b_lin, gn_weight, gn_bias, gn_alpha)):
+            nc.gpsimd.dma_start(out=prow[8 * i:8 * i + 8, :], in_=vec.rearrange("(j p) -> j p", p=P))
+        nc.gpsimd.tensor_copy(out=ident_bf[:], in_=ident[:])
+
+        asc_ps = bank("asc_ps", [P, 4, P])
+        for t in range(4):
+            nc.tensor.transpose(asc_ps[:, t, :], asc[:, t:512:4], ident[:])
+
+        turned = {}
+
+        def turn(name, groups):
+            ps = bank("turn_%s" % name, [P, len(groups), 2, P])
+            for g, words in enumerate(groups):
+                for u in range(2):
+                    nc.tensor.transpose(ps[:, g, u, :], words[:, u:256:2], ident[:])
+            turned[name] = ps
+
+        def agg_src(a):
+            i = min(a // 2, 2)
+            return agg_u8[i][:, 512 * (a - 2 * i):512 * (a - 2 * i + 1)].bitcast(E4M3)
+
+        def widen_s(a):
+            nc.scalar.copy(out=aggw[:, a, :], in_=agg_src(a))
+
+        def widen_v(a):
+            nc.vector.tensor_copy(out=aggw[:, a, :], in_=agg_src(a))
+
+        def turn_agg(a):
+            turn(a, [aggw[:, a, :].bitcast(F32)])
+
+        def scale_agg(a):
+            src = turned[a][:].bitcast(BF16)[:, 0].rearrange("p u (t e) -> p t u e", e=2)
+            fac = s_col[:, a, :].rearrange("p (u e) -> p u e", e=2).unsqueeze(1).to_broadcast([P, T, 2, 2])
+            nc.vector.tensor_tensor(out=grouped[:, GX + a, :].rearrange("p (t u e) -> p t u e", u=2, e=2),
+                                    in0=src, in1=fac, op=MULT)
+
+        def quantize(g, n):
+            nc.vector.quantize_mx(
+                out=codes[:, g:g + n, :].rearrange("p g t -> p (g t)").bitcast(E4M3X4),
+                scales=planes[:, g:g + n, :].rearrange("p g t -> p (g t)"),
+                in_=grouped[:, g:g + n, :].rearrange("p g k -> p (g k)"))
+
+        acc = [acc_bank("acc%d" % h, [P, 512]) for h in range(2)]
+        order = [2, 3, 4, 5, 0, 1, 6, 7, 8, 9]
+
+        def post_pass(g, h):
+            if g < 8:
+                w = post_w[g // 2][:, g % 2, h * C:(h + 1) * C]
+            else:
+                w = post_wl[h][:, g - 8, :]
+            nc.tensor.matmul_mx(out=acc[h][:], lhsT=codes[:, g, :].bitcast(E4M3X4), lhsT_scale=planes[:, g, :],
+                                rhs=w.bitcast(E2M1X4), rhs_scale=post_sc[:, g, 512 * h:512 * (h + 1)],
+                                start=(g == order[0]), stop=(g == order[-1]))
+
+        bias_bc = sb("bias_bc", [P, C], BF16)
+        b_ps = []
+
+        def bias_rows(h):
+            ps = bank("b_ps%d" % h, [P, 512])
+            nc.tensor.matmul(ps[:], lhsT=ones_bf[:], rhs=brow[:, 512 * h:512 * (h + 1)], start=True, stop=True)
+            b_ps.append(ps)
+
+        def bias_copy(h):
+            nc.scalar.copy(out=bias_bc[:, 512 * h:512 * (h + 1)], in_=b_ps[h][:])
+
+        def turn_x():
+            turn("x", [x_sb[:].bitcast(F32)[:, 256 * g:256 * (g + 1)] for g in range(2)])
+
+        def copy_x():
+            nc.scalar.copy(out=grouped[:, 0:2, :].bitcast(F32).rearrange("p g (t u) -> p g t u", u=2),
+                           in_=turned["x"][:].rearrange("p g u t -> p g t u"))
+
+        widen_v(0)
+        nc.vector.tensor_copy(out=s_col[:], in_=asc_ps[:, :, 0:GA].rearrange("p t g -> p g t"))
+        widen_s(1)
+        turn_agg(0)
+        turn_agg(1)
+        widen_v(2)
+        widen_s(3)
+        turn_agg(2)
+        bias_rows(0)
+        bias_rows(1)
+        scale_agg(0)
+        turn_agg(3)
+        scale_agg(1)
+        widen_s(4)
+        turn_x()
+        turn_agg(4)
+        scale_agg(2)
+        widen_s(5)
+        turn_agg(5)
+        quantize(2, 2)
+        scale_agg(3)
+        widen_s(6)
+        turn_agg(6)
+        scale_agg(4)
+        quantize(4, 2)
+        widen_s(7)
+        scale_agg(5)
+        turn_agg(7)
+        copy_x()
+        bias_copy(0)
+        bias_copy(1)
+        scale_agg(6)
+        quantize(0, 2)
+        quantize(6, 2)
+        scale_agg(7)
+        quantize(8, 2)
+
+        for g in order[:6]:
+            for h in range(2):
+                post_pass(g, h)
+
+        for g in order[6:8]:
+            for h in range(2):
+                post_pass(g, h)
+        for h in range(2):
+            for g in order[8:]:
+                post_pass(g, h)
+
+        p_ps = bank("p_ps", [P, P], BF16)
+        nc.tensor.transpose(p_ps[:], prow[:], ident_bf[:])
+        pcol = sb("pcol", [P, 4, 8], F32)
+        nc.scalar.copy(out=pcol[:].rearrange("p v j -> p (v j)"), in_=p_ps[:, 0:32])
+        oma = sb("oma", [P, 8], F32)
+        nal = sb("nal", [P, 8], F32)
+        c1 = sb("c1", [P, 8], F32)
+        nalw = sb("nalw", [P, 8], F32)
+        c1w = sb("c1w", [P, 8], F32)
+        gn_w = pcol[:, 1, :]
+        gn_b = pcol[:, 2, :]
+        nc.gpsimd.tensor_scalar(out=oma[:], in0=pcol[:, 3, :], scalar1=-1.0, scalar2=1.0, op0=MULT, op1=ADD)
+        nc.gpsimd.tensor_scalar(out=nal[:], in0=pcol[:, 3, :], scalar1=-1.0, scalar2=0.0, op0=MULT, op1=ADD)
+        nc.gpsimd.tensor_tensor(out=c1[:], in0=oma[:], in1=pcol[:, 0, :], op=MULT)
+        nc.gpsimd.tensor_tensor(out=nalw[:], in0=nal[:], in1=gn_w, op=MULT)
+        nc.gpsimd.tensor_tensor(out=c1w[:], in0=c1[:], in1=gn_w, op=MULT)
+
+        h_bf = sb("h_bf", [P, 2, 2, 256], BF16)
+        h_grouped = sb("h_grouped", [P, 2, 512], BF16)
+        h_codes = sb("h_codes", [P, 2, T], U32)
+        h_planes = sb("h_planes", [P, 2, T], U8)
+        h_ps = []
+        for h in range(2):
+            ps = bank("h_ps%d" % h, [P, 2, P])
+            for u in range(2):
+                pairs = "p (w u e) -> p u w e"
+                nc.vector.tensor_tensor(out=h_bf[:, h, u, :].rearrange("p (w e) -> p w e", e=2),
+                                        in0=acc[h][:].rearrange(pairs, u=2, e=2)[:, u],
+                                        in1=bias_bc[:, 512 * h:512 * (h + 1)].rearrange(pairs, u=2, e=2)[:, u], op=ADD)
+                nc.tensor.transpose(ps[:, u, :], h_bf[:, h, u, :].bitcast(F32), ident[:])
+            h_ps.append(ps)
+        for h in range(2):
+            nc.scalar.copy(out=h_grouped[:, h, :].bitcast(F32).rearrange("p (t u) -> p t u", u=2),
+                           in_=h_ps[h][:].rearrange("p u t -> p t u"))
+            nc.vector.quantize_mx(out=h_codes[:, h, :].bitcast(E4M3X4), scales=h_planes[:, h, :], in_=h_grouped[:, h, :])
+
+        stats = sb("stats", [P, 8, 8], F32)
+        mv = sb("mv", [P, 8, 2], F32)
+        veps = sb("veps", [P, 8], F32)
+        d2 = sb("d2", [P, 8], F32)
+        ew = sb("ew", [P, 8], F32)
+        rstd = sb("rstd", [P, 8], F32)
+        sc_c = sb("sc_c", [P, 8], F32)
+        bb_c = sb("bb_c", [P, 8], F32)
+        normed = sb("normed", [P, 8, T], F32)
+        result = sb("result", [P, C], F32)
+        o_tiles = [bank("o_ps%d" % k, [P, 2, T]) for k in range(5)]
+        where = [(0, 0), (0, 1), (1, 0), (1, 1), (2, 0), (2, 1), (3, 0), (4, 0)]
+
+        def o_of(j):
+            k, i = where[j]
+            return o_tiles[k][:, i, :]
+
+        def lin_pass(j, g):
+            nc.tensor.matmul_mx(out=o_of(j), lhsT=lin_w[:, g, 256 * j:256 * (j + 1)].bitcast(E2M1X4),
+                                lhsT_scale=lin_sc[:, g, P * j:P * (j + 1)],
+                                rhs=h_codes[:, g, :].bitcast(E4M3X4), rhs_scale=h_planes[:, g, :],
+                                start=(g == 0), stop=(g == 1))
+
+        def col(t, j):
+            return t[:, j:j + 1]
+
+        def st_stats(j):
+            nc.vector.bn_stats(out=stats[:, j, 0:6], in_=o_of(j))
+
+        def st_aggr(j):
+            nc.vector.bn_aggr(out=mv[:, j, :], in_=stats[:, j, 0:6])
+
+        def st_veps(j, n):
+            nc.vector.tensor_scalar(out=veps[:, j:j + n], in0=mv[:, j:j + n, 1], scalar1=EPS, scalar2=None, op0=ADD)
+
+        def st_square(j):
+            nc.scalar.activation(out=col(d2, j), in_=mv[:, j, 0:1], func=ACT.Square, scale=col(oma, j), bias=col(c1, j))
+
+        def st_ew(j):
+            nc.gpsimd.tensor_scalar(out=col(ew, j), in0=mv[:, j, 0:1], scalar1=col(nalw, j), scalar2=col(c1w, j), op0=MULT, op1=ADD)
+
+        def st_rstd(j):
+            nc.scalar.activation(out=col(rstd, j), in_=col(d2, j), func=ACT.Abs_reciprocal_sqrt, bias=col(veps, j))
+
+        def st_sc(j, n, on_scalar):
+            if on_scalar:
+                nc.scalar.activation(out=col(sc_c, j), in_=col(rstd, j), func=ACT.Copy, scale=gn_w[:, j:j + 1])
+            else:
+                nc.vector.tensor_tensor(out=sc_c[:, j:j + n], in0=rstd[:, j:j + n], in1=gn_w[:, j:j + n], op=MULT)
+
+        def st_bb(j):
+            nc.scalar.activation(out=col(bb_c, j), in_=col(rstd, j), func=ACT.Identity, scale=col(ew, j), bias=gn_b[:, j:j + 1])
+
+        def st_norm(j, on_scalar):
+            if on_scalar:
+                nc.scalar.activation(out=normed[:, j, :], in_=o_of(j), func=ACT.Identity, scale=col(sc_c, j), bias=col(bb_c, j))
+            else:
+                nc.vector.tensor_scalar(out=normed[:, j, :], in0=o_of(j), scalar1=col(sc_c, j), scalar2=col(bb_c, j),
+                                        op0=MULT, op1=ADD)
+
+        fins = {}
+
+        def turn_back(k):
+            js = [j for j in range(8) if where[j][0] == k]
+            ps = acc_bank("fin%d" % k, [P, len(js), P]) if k < 2 else bank("fin%d" % k, [P, len(js), P])
+            for i, j in enumerate(js):
+                nc.tensor.transpose(ps[:, i, :], normed[:, j, :], ident[:])
+            fins[k] = (ps, slice(P * js[0], P * (js[-1] + 1)))
+
+        def finish(k):
+            ps, cols = fins[k]
+            nc.vector.scalar_tensor_tensor(out=result[:, cols], in0=ps[:].rearrange("p i c -> p (i c)"), scalar=0.0,
+                                           in1=x_sb[:, cols], op0=MAX, op1=ADD)
+            nc.sync.dma_start(out=out_rows[:, cols], in_=result[:, cols])
+
+        early = (0, 2, 4, 6, 7)
+        for j in early:
+            lin_pass(j, 0)
+        for j in range(8):
+            if j not in early:
+                lin_pass(j, 0)
+            lin_pass(j, 1)
+        for s in range(8 + 1):
+            if s < 8:
+                st_stats(s)
+            if s >= 1:
+                st_aggr(s - 1)
+                st_ew(s - 1)
+            if s in (3, 5, 7):
+                st_veps(s - 3, 2)
+        st_veps(6, 2)
+        for s in range(8 + 3):
+            if s < 8:
+                st_square(s)
+            if 0 <= s - 1 < 8:
+                st_rstd(s - 1)
+            if 0 <= s - 2 < 8:
+                st_bb(s - 2)
+                if s - 2 in (0, 1, 4, 5, 6):
+                    st_sc(s - 2, 1, True)
+            if s - 3 in (0, 1):
+                st_norm(s - 3, True)
+        turn_back(0)
+        st_sc(2, 2, False)
+        st_norm(2, False)
+        st_norm(3, False)
+        st_norm(4, True)
+        st_norm(5, True)
+        st_norm(6, True)
+        st_sc(7, 1, False)
+        st_norm(7, False)
+        finish(0)
+        turn_back(1)
+        turn_back(2)
+        turn_back(3)
+        turn_back(4)
+        finish(1)
+        finish(2)
+        finish(3)
+        finish(4)

@@ -38,14 +38,14 @@ def tile_gnnlayer_pb_w4_kernel(tc, x, agg_bytes, agg_scale, W_post_words, W_post
 
     with ExitStack() as ctx:
         keep = ctx.enter_context(tc.tile_pool(name="keep", bufs=1))
-        psum = ctx.enter_context(tc.psum_pool(name="psum", bufs=6))
+        psum = ctx.enter_context(tc.psum_pool(name="psum", bufs=5))
         ctx.enter_context(tc.manual_schedule())
 
         def sb(name, shape, dtype):
             return keep.tile(shape, dtype, name=name, align_bytes=64)
 
         def bank(name, shape, dtype=F32):
-            return psum.tile(shape, dtype, name=name, tag="bank", bufs=6)
+            return psum.tile(shape, dtype, name=name, tag="bank", bufs=5)
 
         def acc_bank(name, shape):
             return psum.tile(shape, F32, name=name, tag="acc", bufs=2)
@@ -71,10 +71,16 @@ def tile_gnnlayer_pb_w4_kernel(tc, x, agg_bytes, agg_scale, W_post_words, W_post
         post_wl = [sb("post_wl%d" % h, [P, 2, C], U8) for h in range(2)]
         lin_w = sb("lin_w", [P, 2, 2 * C], U8)
 
-        nc.gpsimd.memset(brow[:].bitcast(I32), 0)
+        make_identity(nc, ident[:])
         nc.vector.memset(asc[:], 0.0)
+        nc.vector.memset(brow[:].bitcast(I32), 0)
         nc.vector.memset(warm[:], 1.0)
         nc.vector.memset(ones_bf[:], 1.0)
+        nc.vector.memset(post_sc[:].bitcast(I32), 0)
+        nc.gpsimd.memset(prow[:], 0.0)
+        nc.gpsimd.memset(lin_sc[:].bitcast(I32), 0)
+        nc.gpsimd.tensor_copy(out=ident_bf[:], in_=ident[:])
+
         nc.sync.dma_start(out=agg_u8[0][:], in_=agg_rows[:, 0:1024])
         nc.sync.dma_start(out=asc[0:GA, :], in_=asc_rows)
         nc.sync.dma_start(out=agg_u8[1][:], in_=agg_rows[:, 1024:2048])
@@ -82,24 +88,26 @@ def tile_gnnlayer_pb_w4_kernel(tc, x, agg_bytes, agg_scale, W_post_words, W_post
         nc.scalar.dma_start(out=brow[0:1, :], in_=b_post.rearrange("(o c) -> o c", o=1))
         nc.scalar.activation(out=warm2[:], in_=warm[:], func=ACT.Abs_reciprocal_sqrt)
         nc.sync.dma_start(out=x_sb[:], in_=x_rows)
-        nc.vector.memset(post_sc[:].bitcast(I32), 0)
-        nc.vector.memset(lin_sc[:].bitcast(I32), 0)
         for r in range(4):
             nc.sync.dma_start(out=post_sc[r:128:32, :, :].bitcast(I32), in_=wps[r])
         for i in (1, 2, 0, 3):
             nc.sync.dma_start(out=post_w[i][:], in_=W_post_words[2 * i:2 * i + 2].rearrange("g p n -> p g n"))
+            if i == 2:
+                for v, vec in enumerate((b_lin, gn_weight, gn_bias, gn_alpha)):
+                    nc.sync.dma_start(out=prow[8 * v:8 * v + 8, :], in_=vec.rearrange("(j p) -> j p", p=P))
         for h in range(2):
             nc.sync.dma_start(out=post_wl[h][:], in_=W_post_words[8:10, :, h * C:(h + 1) * C].rearrange("g p n -> p g n"))
         for r in range(4):
             nc.sync.dma_start(out=lin_sc[r:128:32, :, :].bitcast(I32), in_=wls[r])
         nc.sync.dma_start(out=lin_w[:], in_=W_lin_words.rearrange("g p n -> p g n"))
 
-        make_identity(nc, ident[:])
-        nc.gpsimd.memset(prow[:], 0.0)
-        for i, vec in enumerate((b_lin, gn_weight, gn_bias, gn_alpha)):
-            nc.gpsimd.dma_start(out=prow[8 * i:8 * i + 8, :], in_=vec.rearrange("(j p) -> j p", p=P))
-        nc.gpsimd.tensor_copy(out=ident_bf[:], in_=ident[:])
+        scratch = psum.tile([P, P], F32, name="scratch", tag="scratch", bufs=1)
 
+        def keep_warm(n):
+            for i in range(n):
+                nc.tensor.matmul(scratch[:], lhsT=ident[:], rhs=ident[:], start=True, stop=True)
+
+        keep_warm(4)
         asc_ps = bank("asc_ps", [P, 4, P])
         for t in range(4):
             nc.tensor.transpose(asc_ps[:, t, :], asc[:, t:512:4], ident[:])
@@ -125,6 +133,8 @@ def tile_gnnlayer_pb_w4_kernel(tc, x, agg_bytes, agg_scale, W_post_words, W_post
 
         def turn_agg(a):
             turn(a, [aggw[:, a, :].bitcast(F32)])
+            if a in (1, 3, 5):
+                keep_warm(2)
 
         def scale_agg(a):
             src = turned[a][:].bitcast(BF16)[:, 0].rearrange("p u (t e) -> p t u e", e=2)
@@ -176,8 +186,6 @@ def tile_gnnlayer_pb_w4_kernel(tc, x, agg_bytes, agg_scale, W_post_words, W_post
         widen_v(2)
         widen_s(3)
         turn_agg(2)
-        bias_rows(0)
-        bias_rows(1)
         scale_agg(0)
         turn_agg(3)
         scale_agg(1)
@@ -197,6 +205,8 @@ def tile_gnnlayer_pb_w4_kernel(tc, x, agg_bytes, agg_scale, W_post_words, W_post
         scale_agg(5)
         turn_agg(7)
         copy_x()
+        bias_rows(0)
+        bias_rows(1)
         bias_copy(0)
         bias_copy(1)
         scale_agg(6)
@@ -207,13 +217,6 @@ def tile_gnnlayer_pb_w4_kernel(tc, x, agg_bytes, agg_scale, W_post_words, W_post
 
         for g in order[:6]:
             for h in range(2):
-                post_pass(g, h)
-
-        for g in order[6:8]:
-            for h in range(2):
-                post_pass(g, h)
-        for h in range(2):
-            for g in order[8:]:
                 post_pass(g, h)
 
         p_ps = bank("p_ps", [P, P], BF16)
@@ -232,6 +235,13 @@ def tile_gnnlayer_pb_w4_kernel(tc, x, agg_bytes, agg_scale, W_post_words, W_post
         nc.gpsimd.tensor_tensor(out=c1[:], in0=oma[:], in1=pcol[:, 0, :], op=MULT)
         nc.gpsimd.tensor_tensor(out=nalw[:], in0=nal[:], in1=gn_w, op=MULT)
         nc.gpsimd.tensor_tensor(out=c1w[:], in0=c1[:], in1=gn_w, op=MULT)
+
+        for g in order[6:8]:
+            for h in range(2):
+                post_pass(g, h)
+        for h in range(2):
+            for g in order[8:]:
+                post_pass(g, h)
 
         h_bf = sb("h_bf", [P, 2, 2, 256], BF16)
         h_grouped = sb("h_grouped", [P, 2, 512], BF16)
@@ -327,13 +337,16 @@ def tile_gnnlayer_pb_w4_kernel(tc, x, agg_bytes, agg_scale, W_post_words, W_post
                                            in1=x_sb[:, cols], op0=MAX, op1=ADD)
             nc.sync.dma_start(out=out_rows[:, cols], in_=result[:, cols])
 
+        keep_warm(2)
         early = (0, 2, 4, 6, 7)
         for j in early:
             lin_pass(j, 0)
+        keep_warm(1)
         for j in range(8):
             if j not in early:
                 lin_pass(j, 0)
             lin_pass(j, 1)
+        keep_warm(4)
         for s in range(8 + 1):
             if s < 8:
                 st_stats(s)

from contextlib import ExitStack

import concourse.mybir as mybir
from concourse.masks import make_identity

F32 = mybir.dt.float32
BF16 = mybir.dt.bfloat16
U32 = mybir.dt.uint32
I32 = mybir.dt.int32
U8 = mybir.dt.uint8
E4M3 = mybir.dt.float8_e4m3fn
E4M3X4 = mybir.dt.float8_e4m3fn_x4
E2M1X4 = mybir.dt.float4_e2m1fn_x4
ADD = mybir.AluOpType.add
MULT = mybir.AluOpType.mult
MAX = mybir.AluOpType.max
ACT = mybir.ActivationFunctionType

P = 128
T = 128
C = 1024
GX = 2
GA = 8
G = GX + GA
EPS = 1e-5
FLOPS = 2 * T * (G * 512 + C) * C


def tile_gnnlayer_pb_w4_kernel(tc, x, agg_bytes, agg_scale, W_post_words, W_post_scales, b_post,
                                           W_lin_words, W_lin_scales, b_lin, gn_weight, gn_bias, gn_alpha, out):
    nc = tc.nc
    x_rows = x.rearrange("b n c -> (b n) c")
    agg_rows = agg_bytes.rearrange("b n k -> (b n) k")
    out_rows = out.rearrange("b n c -> (b n) c")
    asc_rows = agg_scale.rearrange("o b (g c) -> (o b g) c", g=GA)
    wps = W_post_scales.bitcast(I32).rearrange("g (q r) n -> r q g n", r=4)
    wls = W_lin_scales.bitcast(I32).rearrange("g (q r) n -> r q g n", r=4)

    with ExitStack() as ctx:
        keep = ctx.enter_context(tc.tile_pool(name="keep", bufs=1))
        psum = ctx.enter_context(tc.psum_pool(name="psum", bufs=5))
        ctx.enter_context(tc.manual_schedule())

        def sb(name, shape, dtype):
            return keep.tile(shape, dtype, name=name, align_bytes=64)

        def bank(name, shape, dtype=F32):
            return psum.tile(shape, dtype, name=name, tag="bank", bufs=5)

        def acc_bank(name, shape):
            return psum.tile(shape, F32, name=name, tag="acc", bufs=2)

        asc = sb("asc", [P, 512], F32)
        warm = sb("warm", [P, 1], F32)
        warm2 = sb("warm2", [P, 1], F32)
        ident = sb("ident", [P, P], F32)
        ident_bf = sb("ident_bf", [P, P], BF16)
        ones_bf = sb("ones_bf", [P, P], BF16)
        prow = sb("prow", [P, P], BF16)
        brow = sb("brow", [P, C], BF16)
        x_sb = sb("x_sb", [P, C], BF16)
        agg_u8 = [sb("agg_u8_%d" % i, [P, n], U8) for i, n in enumerate((1024, 1024, 2048))]
        aggw = sb("aggw", [P, GA, 512], BF16)
        s_col = sb("s_col", [P, GA, 4], F32)
        grouped = sb("grouped", [P, G, 512], BF16)
        codes = sb("codes", [P, G, T], U32)
        planes = sb("planes", [P, G, T], U8)
        post_sc = sb("post_sc", [P, G, C], U8)
        lin_sc = sb("lin_sc", [P, 2, C], U8)
        post_w = [sb("post_w%d" % i, [P, 2, 2 * C], U8) for i in range(4)]
        post_wl = [sb("post_wl%d" % h, [P, 2, C], U8) for h in range(2)]
        lin_w = sb("lin_w", [P, 2, 2 * C], U8)

        make_identity(nc, ident[:])
        nc.vector.memset(asc[:], 0.0)
        nc.vector.memset(brow[:].bitcast(I32), 0)
        nc.vector.memset(warm[:], 1.0)
        nc.vector.memset(ones_bf[:], 1.0)
        nc.vector.memset(post_sc[:].bitcast(I32), 0)
        nc.gpsimd.memset(prow[:], 0.0)
        nc.gpsimd.memset(lin_sc[:].bitcast(I32), 0)
        nc.gpsimd.tensor_copy(out=ident_bf[:], in_=ident[:])

        nc.sync.dma_start(out=agg_u8[0][:], in_=agg_rows[:, 0:1024])
        nc.sync.dma_start(out=asc[0:GA, :], in_=asc_rows)
        nc.sync.dma_start(out=agg_u8[1][:], in_=agg_rows[:, 1024:2048])
        nc.sync.dma_start(out=agg_u8[2][:], in_=agg_rows[:, 2048:4096])
        nc.scalar.dma_start(out=brow[0:1, :], in_=b_post.rearrange("(o c) -> o c", o=1))
        nc.scalar.activation(out=warm2[:], in_=warm[:], func=ACT.Abs_reciprocal_sqrt)
        nc.sync.dma_start(out=x_sb[:], in_=x_rows)
        for r in range(4):
            nc.sync.dma_start(out=post_sc[r:128:32, :, :].bitcast(I32), in_=wps[r])
        for i in (1, 2, 0, 3):
            nc.sync.dma_start(out=post_w[i][:], in_=W_post_words[2 * i:2 * i + 2].rearrange("g p n -> p g n"))
            if i == 2:
                for v, vec in enumerate((b_lin, gn_weight, gn_bias, gn_alpha)):
                    nc.sync.dma_start(out=prow[8 * v:8 * v + 8, :], in_=vec.rearrange("(j p) -> j p", p=P))
        for h in range(2):
            nc.sync.dma_start(out=post_wl[h][:], in_=W_post_words[8:10, :, h * C:(h + 1) * C].rearrange("g p n -> p g n"))
        for r in range(4):
            nc.sync.dma_start(out=lin_sc[r:128:32, :, :].bitcast(I32), in_=wls[r])
        nc.sync.dma_start(out=lin_w[:], in_=W_lin_words.rearrange("g p n -> p g n"))

        scratch = psum.tile([P, P], F32, name="scratch", tag="scratch", bufs=1)

        def keep_warm(n):
            for i in range(n):
                nc.tensor.matmul(scratch[:], lhsT=ident[:], rhs=ident[:], start=True, stop=True)

        keep_warm(4)
        asc_ps = bank("asc_ps", [P, 4, P])
        for t in range(4):
            nc.tensor.transpose(asc_ps[:, t, :], asc[:, t:512:4], ident[:])

        turned = {}

        def turn(name, groups):
            ps = bank("turn_%s" % name, [P, len(groups), 2, P])
            for g, words in enumerate(groups):
                for u in range(2):
                    nc.tensor.transpose(ps[:, g, u, :], words[:, u:256:2], ident[:])
            turned[name] = ps

        def agg_src(a):
            i = min(a // 2, 2)
            return agg_u8[i][:, 512 * (a - 2 * i):512 * (a - 2 * i + 1)].bitcast(E4M3)

        def widen_s(a):
            nc.scalar.copy(out=aggw[:, a, :], in_=agg_src(a))

        def widen_v(a):
            nc.vector.tensor_copy(out=aggw[:, a, :], in_=agg_src(a))

        def turn_agg(a):
            turn(a, [aggw[:, a, :].bitcast(F32)])
            if a in (1, 3, 5):
                keep_warm(2)

        def scale_agg(a):
            src = turned[a][:].bitcast(BF16)[:, 0].rearrange("p u (t e) -> p t u e", e=2)
            fac = s_col[:, a, :].rearrange("p (u e) -> p u e", e=2).unsqueeze(1).to_broadcast([P, T, 2, 2])
            nc.vector.tensor_tensor(out=grouped[:, GX + a, :].rearrange("p (t u e) -> p t u e", u=2, e=2),
                                    in0=src, in1=fac, op=MULT)

        def quantize(g, n):
            nc.vector.quantize_mx(
                out=codes[:, g:g + n, :].rearrange("p g t -> p (g t)").bitcast(E4M3X4),
                scales=planes[:, g:g + n, :].rearrange("p g t -> p (g t)"),
                in_=grouped[:, g:g + n, :].rearrange("p g k -> p (g k)"))

        acc = [acc_bank("acc%d" % h, [P, 512]) for h in range(2)]
        order = [2, 3, 4, 5, 0, 1, 6, 7, 8, 9]

        def post_pass(g, h):
            if g < 8:
                w = post_w[g // 2][:, g % 2, h * C:(h + 1) * C]
            else:
                w = post_wl[h][:, g - 8, :]
            nc.tensor.matmul_mx(out=acc[h][:], lhsT=codes[:, g, :].bitcast(E4M3X4), lhsT_scale=planes[:, g, :],
                                rhs=w.bitcast(E2M1X4), rhs_scale=post_sc[:, g, 512 * h:512 * (h + 1)],
                                start=(g == order[0]), stop=(g == order[-1]))

        bias_bc = sb("bias_bc", [P, C], BF16)
        b_ps = []

        def bias_rows(h):
            ps = bank("b_ps%d" % h, [P, 512])
            nc.tensor.matmul(ps[:], lhsT=ones_bf[:], rhs=brow[:, 512 * h:512 * (h + 1)], start=True, stop=True)
            b_ps.append(ps)

        def bias_copy(h):
            nc.scalar.copy(out=bias_bc[:, 512 * h:512 * (h + 1)], in_=b_ps[h][:])

        def turn_x():
            turn("x", [x_sb[:].bitcast(F32)[:, 256 * g:256 * (g + 1)] for g in range(2)])

        def copy_x():
            nc.scalar.copy(out=grouped[:, 0:2, :].bitcast(F32).rearrange("p g (t u) -> p g t u", u=2),
                           in_=turned["x"][:].rearrange("p g u t -> p g t u"))

        widen_v(0)
        nc.vector.tensor_copy(out=s_col[:], in_=asc_ps[:, :, 0:GA].rearrange("p t g -> p g t"))
        widen_s(1)
        turn_agg(0)
        turn_agg(1)
        widen_v(2)
        widen_s(3)
        turn_agg(2)
        scale_agg(0)
        turn_agg(3)
        scale_agg(1)
        widen_s(4)
        turn_x()
        turn_agg(4)
        scale_agg(2)
        widen_s(5)
        turn_agg(5)
        quantize(2, 2)
        scale_agg(3)
        widen_s(6)
        turn_agg(6)
        scale_agg(4)
        quantize(4, 2)
        widen_s(7)
        scale_agg(5)
        turn_agg(7)
        copy_x()
        bias_rows(0)
        bias_rows(1)
        bias_copy(0)
        bias_copy(1)
        scale_agg(6)
        quantize(0, 2)
        quantize(6, 2)
        scale_agg(7)
        quantize(8, 2)

        for g in order[:6]:
            for h in range(2):
                post_pass(g, h)

        p_ps = bank("p_ps", [P, P], BF16)
        nc.tensor.transpose(p_ps[:], prow[:], ident_bf[:])
        pcol = sb("pcol", [P, 4, 8], F32)
        nc.scalar.copy(out=pcol[:].rearrange("p v j -> p (v j)"), in_=p_ps[:, 0:32])
        oma = sb("oma", [P, 8], F32)
        nal = sb("nal", [P, 8], F32)
        c1 = sb("c1", [P, 8], F32)
        nalw = sb("nalw", [P, 8], F32)
        c1w = sb("c1w", [P, 8], F32)
        gn_w = pcol[:, 1, :]
        gn_b = pcol[:, 2, :]
        nc.gpsimd.tensor_scalar(out=oma[:], in0=pcol[:, 3, :], scalar1=-1.0, scalar2=1.0, op0=MULT, op1=ADD)
        nc.gpsimd.tensor_scalar(out=nal[:], in0=pcol[:, 3, :], scalar1=-1.0, scalar2=0.0, op0=MULT, op1=ADD)
        nc.gpsimd.tensor_tensor(out=c1[:], in0=oma[:], in1=pcol[:, 0, :], op=MULT)
        nc.gpsimd.tensor_tensor(out=nalw[:], in0=nal[:], in1=gn_w, op=MULT)
        nc.gpsimd.tensor_tensor(out=c1w[:], in0=c1[:], in1=gn_w, op=MULT)

        for g in order[6:8]:
            for h in range(2):
                post_pass(g, h)
        for h in range(2):
            for g in order[8:]:
                post_pass(g, h)

        h_bf = sb("h_bf", [P, 2, 2, 256], BF16)
        h_grouped = sb("h_grouped", [P, 2, 512], BF16)
        h_codes = sb("h_codes", [P, 2, T], U32)
        h_planes = sb("h_planes", [P, 2, T], U8)
        h_ps = []
        for h in range(2):
            ps = bank("h_ps%d" % h, [P, 2, P])
            for u in range(2):
                pairs = "p (w u e) -> p u w e"
                nc.vector.tensor_tensor(out=h_bf[:, h, u, :].rearrange("p (w e) -> p w e", e=2),
                                        in0=acc[h][:].rearrange(pairs, u=2, e=2)[:, u],
                                        in1=bias_bc[:, 512 * h:512 * (h + 1)].rearrange(pairs, u=2, e=2)[:, u], op=ADD)
                nc.tensor.transpose(ps[:, u, :], h_bf[:, h, u, :].bitcast(F32), ident[:])
            h_ps.append(ps)
        for h in range(2):
            nc.scalar.copy(out=h_grouped[:, h, :].bitcast(F32).rearrange("p (t u) -> p t u", u=2),
                           in_=h_ps[h][:].rearrange("p u t -> p t u"))
            nc.vector.quantize_mx(out=h_codes[:, h, :].bitcast(E4M3X4), scales=h_planes[:, h, :], in_=h_grouped[:, h, :])

        stats = sb("stats", [P, 8, 8], F32)
        mv = sb("mv", [P, 8, 2], F32)
        veps = sb("veps", [P, 8], F32)
        d2 = sb("d2", [P, 8], F32)
        ew = sb("ew", [P, 8], F32)
        rstd = sb("rstd", [P, 8], F32)
        sc_c = sb("sc_c", [P, 8], F32)
        bb_c = sb("bb_c", [P, 8], F32)
        normed = sb("normed", [P, 8, T], F32)
        result = sb("result", [P, C], F32)
        o_tiles = [bank("o_ps%d" % k, [P, 2, T]) for k in range(5)]
        where = [(0, 0), (0, 1), (1, 0), (1, 1), (2, 0), (2, 1), (3, 0), (4, 0)]

        def o_of(j):
            k, i = where[j]
            return o_tiles[k][:, i, :]

        def lin_pass(j, g):
            nc.tensor.matmul_mx(out=o_of(j), lhsT=lin_w[:, g, 256 * j:256 * (j + 1)].bitcast(E2M1X4),
                                lhsT_scale=lin_sc[:, g, P * j:P * (j + 1)],
                                rhs=h_codes[:, g, :].bitcast(E4M3X4), rhs_scale=h_planes[:, g, :],
                                start=(g == 0), stop=(g == 1))

        def col(t, j):
            return t[:, j:j + 1]

        def st_stats(j):
            nc.vector.bn_stats(out=stats[:, j, 0:6], in_=o_of(j))

        def st_aggr(j):
            nc.vector.bn_aggr(out=mv[:, j, :], in_=stats[:, j, 0:6])

        def st_veps(j, n):
            nc.vector.tensor_scalar(out=veps[:, j:j + n], in0=mv[:, j:j + n, 1], scalar1=EPS, scalar2=None, op0=ADD)

        def st_square(j):
            nc.scalar.activation(out=col(d2, j), in_=mv[:, j, 0:1], func=ACT.Square, scale=col(oma, j), bias=col(c1, j))

        def st_ew(j):
            nc.gpsimd.tensor_scalar(out=col(ew, j), in0=mv[:, j, 0:1], scalar1=col(nalw, j), scalar2=col(c1w, j), op0=MULT, op1=ADD)

        def st_rstd(j):
            nc.scalar.activation(out=col(rstd, j), in_=col(d2, j), func=ACT.Abs_reciprocal_sqrt, bias=col(veps, j))

        def st_sc(j, n, on_scalar):
            if on_scalar:
                nc.scalar.activation(out=col(sc_c, j), in_=col(rstd, j), func=ACT.Copy, scale=gn_w[:, j:j + 1])
            else:
                nc.vector.tensor_tensor(out=sc_c[:, j:j + n], in0=rstd[:, j:j + n], in1=gn_w[:, j:j + n], op=MULT)

        def st_bb(j):
            nc.scalar.activation(out=col(bb_c, j), in_=col(rstd, j), func=ACT.Identity, scale=col(ew, j), bias=gn_b[:, j:j + 1])

        def st_norm(j, on_scalar):
            if on_scalar:
                nc.scalar.activation(out=normed[:, j, :], in_=o_of(j), func=ACT.Identity, scale=col(sc_c, j), bias=col(bb_c, j))
            else:
                nc.vector.tensor_scalar(out=normed[:, j, :], in0=o_of(j), scalar1=col(sc_c, j), scalar2=col(bb_c, j),
                                        op0=MULT, op1=ADD)

        fins = {}

        def turn_back(k):
            js = [j for j in range(8) if where[j][0] == k]
            ps = acc_bank("fin%d" % k, [P, len(js), P]) if k < 2 else bank("fin%d" % k, [P, len(js), P])
            for i, j in enumerate(js):
                nc.tensor.transpose(ps[:, i, :], normed[:, j, :], ident[:])
            fins[k] = (ps, slice(P * js[0], P * (js[-1] + 1)))

        def finish(k):
            ps, cols = fins[k]
            nc.vector.scalar_tensor_tensor(out=result[:, cols], in0=ps[:].rearrange("p i c -> p (i c)"), scalar=0.0,
                                           in1=x_sb[:, cols], op0=MAX, op1=ADD)
            nc.sync.dma_start(out=out_rows[:, cols], in_=result[:, cols])

        keep_warm(2)
        early = (0, 2, 4, 6, 7)
        for j in early:
            lin_pass(j, 0)
        keep_warm(1)
        for j in range(8):
            if j not in early:
                lin_pass(j, 0)
            lin_pass(j, 1)
        keep_warm(4)
        for s in range(8 + 1):
            if s < 8:
                st_stats(s)
            if s >= 1:
                st_aggr(s - 1)
                st_ew(s - 1)
            if s in (3, 5, 7):
                st_veps(s - 3, 2)
        st_veps(6, 2)
        for s in range(8 + 3):
            if s < 8:
                st_square(s)
            if 0 <= s - 1 < 8:
                st_rstd(s - 1)
            if 0 <= s - 2 < 8:
                st_bb(s - 2)
                if s - 2 in (0, 1, 4, 5, 6):
                    st_sc(s - 2, 1, True)
            if s - 3 in (0, 1):
                st_norm(s - 3, True)
        turn_back(0)
        st_sc(2, 2, False)
        st_norm(2, False)
        st_norm(3, False)
        st_norm(4, True)
        st_norm(5, True)
        st_norm(6, True)
        st_sc(7, 1, False)
        st_norm(7, False)
        finish(0)
        turn_back(1)
        turn_back(2)
        turn_back(3)
        turn_back(4)
        finish(1)
        finish(2)
        finish(3)
        finish(4)
